import numpy as np
import ml_dtypes


def mxq(x, axis, fmt="e4m3"):
    dtype, down = {"e4m3": (ml_dtypes.float8_e4m3fn, 7), "e5m2": (ml_dtypes.float8_e5m2, 14)}[fmt]
    v = np.moveaxis(np.asarray(x, np.float32).astype(ml_dtypes.bfloat16).astype(np.float64), axis, -1)
    blocks = v.reshape(v.shape[:-1] + (-1, 32))
    amax = np.abs(blocks).max(-1, keepdims=True)
    byte = np.maximum(np.where(amax > 0, np.frexp(amax)[1] - 1 + 127, 0) - down, 1)
    scale = np.exp2(byte - 127.0)
    codes = (blocks / scale).astype(np.float32).astype(dtype).astype(np.float64)
    return np.moveaxis((codes * scale).reshape(v.shape), -1, axis)


WIDE = False


def mx_kscale(k):
    if not WIDE:
        return np.ones(k)
    levels = np.array([18, -18])
    if k % 512:
        return np.exp2(np.random.permutation(np.resize(levels, k // 32))).repeat(32)
    a = np.empty((k // 512, 16))
    for p in range(k // 512):
        a[p, :8] = np.random.permutation(np.resize(levels, 8))
        for g in range(8):
            far = levels[np.abs(levels - a[p, g]) >= 10]
            a[p, g + 8] = far[np.random.randint(len(far))]
    return np.exp2(a.ravel()).repeat(32)


BF16 = ml_dtypes.bfloat16


def bf(x):
    return np.asarray(x, np.float32).astype(BF16)


def f64(x):
    return np.asarray(x).astype(np.float64)


B, D = 1024, 1024
F2 = 2 * D
F3 = D
KMIN = 0.5
KMAX = 2.0


def limits(x0, x1):
    pos = x1 > 0
    num = np.maximum(x0 - KMIN * x1, 0.0) * np.maximum(KMAX * x1 - x0, 0.0)
    denom = (x1 * KMIN) ** 2
    safe_denom = np.where(pos, denom, 1.0)
    lim = np.where(pos, num / safe_denom, 0.0)
    return lim[:, None]


def setup_inputs():
    s = mx_kscale(B)[:, None]
    u = mx_kscale(D)
    v = mx_kscale(F3)
    x1 = 1.0 + 0.6 * np.random.standard_normal(B)
    x1 = np.where(np.random.random(B) < 0.05, 0.0, x1)
    x0 = 1.2 + 0.7 * np.random.standard_normal(B)
    h2_0 = bf(np.tanh(np.random.standard_normal((B, F2))))
    W3_0 = bf(np.random.standard_normal((F3, F2)) * 1.5 / np.sqrt(F2))
    b3 = bf(np.random.standard_normal(F3) * 0.3)
    W4_0 = bf(np.random.standard_normal((D, F3)) * 2.0 / np.sqrt(F3))
    b4 = bf(np.random.standard_normal(D) * 0.5)
    g = bf(np.random.standard_normal((B, D)) * np.exp2(np.random.randint(-6, 1, (B, 1))) / s * u)
    h3 = np.tanh(f64(h2_0) @ f64(W3_0).T + f64(b3))
    y = h3 @ f64(W4_0).T + f64(b4)
    return {"h2": bf(f64(h2_0) * s),
            "W3": bf(f64(W3_0) / v[:, None]),
            "b3": b3,
            "W4": bf(f64(W4_0) * v[None, :] / u[:, None]),
            "b4": b4,
            "x0": bf(x0), "x1": bf(x1),
            "h3": np.asarray(h3, np.float32),
            "y": np.asarray(y, np.float32),
            "grad_out": g}


def reference(h2, W3, b3, W4, b4, x0, x1, h3, y, grad_out):
    lim = limits(f64(x0), f64(x1))
    dz2 = f64(grad_out) * (2.0 * f64(y) * lim)
    dh = mxq(dz2, 1, "e5m2") @ mxq(f64(W4), 0, "e4m3")
    dz1 = dh * (1.0 - f64(h3) ** 2)
    dh2 = mxq(dz1, 1, "e5m2") @ mxq(f64(W3), 0, "e4m3")
    dW3 = mxq(dz1, 0, "e5m2").T @ mxq(f64(h2), 0, "e4m3")
    return dh2, dW3

@@ -1,0 +1,307 @@
+from contextlib import ExitStack
+
+import concourse.mybir as mybir
+from concourse.masks import make_identity
+
+FLOPS = 2 * 1024 * 1024 * 1024 + 2 * 2 * 1024 * 1024 * 2048
+BYTES = 2 * (1024 * 2048 * 2 + 1024 * 1024 * 2 + 2 * 1024) + 2 * 4 * 1024 * 1024 + 2 * 4 * 1024 * 2048
+
+F32 = mybir.dt.float32
+BF16 = mybir.dt.bfloat16
+U32 = mybir.dt.uint32
+U8 = mybir.dt.uint8
+E4M3 = mybir.dt.float8_e4m3fn_x4
+E5M2 = mybir.dt.float8_e5m2_x4
+ALU = mybir.AluOpType
+ACT = mybir.ActivationFunctionType
+
+P = 128
+
+
+def tile_mlp_v1_pa_v_kernel(tc, h2, W3, b3, W4, b4, x0, x1, h3, y, grad_out, out_0, out_1):
+    nc = tc.nc
+    V, S, T = nc.vector, nc.scalar, nc.tensor
+    y_v = y.rearrange("(g p j) d -> g p j d", p=P, j=4)
+    g_v = grad_out.rearrange("(g p j) d -> g p j d", p=P, j=4)
+    h3_v = h3.rearrange("(g p j) d -> g p j d", p=P, j=4)
+    W4_v = W4.rearrange("(c p j) f -> c p j f", p=P, j=4)
+    W3_v = W3.rearrange("(c p j) f -> c p j f", p=P, j=4)
+    h2_v = h2.rearrange("(c p j) f -> c p j f", p=P, j=4)
+    o0_v = out_0.rearrange("(g p j) f -> g p j f", p=P, j=4)
+
+    with ExitStack() as ctx:
+        keep = ctx.enter_context(tc.tile_pool(name="keep", bufs=1))
+        raw = ctx.enter_context(tc.tile_pool(name="raw", bufs=13))
+        mid = ctx.enter_context(tc.tile_pool(name="mid", bufs=3))
+        psum = ctx.enter_context(tc.psum_pool(name="psum", bufs=1))
+
+        w4_codes = keep.tile([P, 2, 1024], U32, align_bytes=64)
+        w4_scales = keep.tile([P, 2, 1024], U8, align_bytes=64)
+        w3_codes = keep.tile([P, 2, 2048], U32, align_bytes=64)
+        w3_scales = keep.tile([P, 2, 2048], U8, align_bytes=64)
+        h2_codes = keep.tile([P, 2, 2048], U32, align_bytes=64)
+        h2_scales = keep.tile([P, 2, 2048], U8, align_bytes=64)
+        t1_codes = keep.tile([P, 2, 1024], U32, align_bytes=64)
+        t1_scales = keep.tile([P, 2, 1024], U8, align_bytes=64)
+        ident = keep.tile([P, P], F32)
+        make_identity(nc, ident[:])
+
+        def COPY(eng):
+            return V.tensor_copy if eng == "v" else S.copy
+
+        raws = {}
+
+        def new_raw(name, shape, dtype):
+            chunk = raw.tile(shape, dtype, tag="raw", align_bytes=64)
+            raws[name] = chunk
+            return chunk
+
+        def load_g(g, js):
+            if ("g", g) not in raws:
+                new_raw(("g", g), [P, 4, 1024], BF16)
+            nc.sync.dma_start(out=raws["g", g][:, js, :], in_=g_v[g, :, js, :])
+
+        def load_tok(name, view, g, half, js):
+            key = (name, g, half)
+            if key not in raws:
+                new_raw(key, [P, 2, 1024], F32)
+            nc.sync.dma_start(out=raws[key][:, js, :], in_=view[g, :, slice(2 * half + js.start, 2 * half + js.stop), :])
+
+        def load_w(name, view, c, half):
+            t = new_raw((name, c, half), [P, 4, 1024], BF16)
+            nc.sync.dma_start(out=t[:], in_=view[c, :, :, 1024 * half : 1024 * half + 1024])
+
+        BOTH = slice(0, 2)
+        x0_sb = keep.tile([P, 2, 4], BF16)
+        x1_sb = keep.tile([P, 2, 4], BF16)
+        nc.scalar.dma_start(out=x0_sb[:], in_=x0.rearrange("(g p j) -> p g j", p=P, j=4))
+        nc.scalar.dma_start(out=x1_sb[:], in_=x1.rearrange("(g p j) -> p g j", p=P, j=4))
+        warm = keep.tile([P, 2], F32)
+        V.memset(warm[:], 0.0)
+        S.activation(out=warm[:, 1:2], in_=warm[:, 0:1], func=ACT.Square)
+
+        load_g(0, slice(0, 2))
+        load_tok("y", y_v, 0, 0, slice(0, 1))
+        load_tok("y", y_v, 0, 0, slice(1, 2))
+        load_w("w4", W4_v, 0, 0)
+        load_g(0, slice(2, 4))
+        load_tok("y", y_v, 0, 1, BOTH)
+        load_w("w4", W4_v, 1, 0)
+        load_tok("h3", h3_v, 0, 0, BOTH)
+        load_tok("h3", h3_v, 0, 1, BOTH)
+        for half in range(2):
+            for c in range(2):
+                load_w("w3", W3_v, c, half)
+        load_g(1, slice(0, 4))
+        load_tok("y", y_v, 1, 0, BOTH)
+
+        xa = x0_sb[:].rearrange("p g j -> p (g j)")
+        xb = x1_sb[:].rearrange("p g j -> p (g j)")
+        lim = keep.tile([P, 8, 8], F32)
+        npos, safe, inv, a, a2, b, b2, nf = [lim[:, i, :] for i in range(8)]
+        V.tensor_scalar(out=npos, in0=xb, scalar1=0.0, scalar2=None, op0=ALU.is_le)
+        V.scalar_tensor_tensor(out=a, in0=xb, scalar=-0.5, in1=xa, op0=ALU.mult, op1=ALU.add)
+        V.scalar_tensor_tensor(out=safe, in0=xb, scalar=0.0, in1=npos, op0=ALU.max, op1=ALU.add)
+        V.scalar_tensor_tensor(out=b, in0=xb, scalar=2.0, in1=xa, op0=ALU.mult, op1=ALU.subtract)
+        V.reciprocal(out=inv, in_=safe)
+        V.scalar_tensor_tensor(out=b2, in0=b, scalar=0.0, in1=inv, op0=ALU.max, op1=ALU.mult)
+        V.scalar_tensor_tensor(out=a2, in0=a, scalar=0.0, in1=inv, op0=ALU.max, op1=ALU.mult)
+        V.tensor_scalar(out=b2, in0=b2, scalar1=1.5, scalar2=-8.0, op0=ALU.min, op1=ALU.mult)
+        V.scalar_tensor_tensor(out=nf, in0=a2, scalar=1.5, in1=b2, op0=ALU.min, op1=ALU.mult)
+
+        dz2, dz1, grp, tok, codes2, codes1, stg, wg = {}, {}, {}, {}, {}, {}, {}, {}
+        trb, dhb = {}, {}
+
+        def A(i):
+            g, j = divmod(i, 4)
+            rows = mid.tile([P, 1024], BF16, tag="dz2", bufs=3, align_bytes=64)
+            dz2[i] = rows
+            V.scalar_tensor_tensor(out=dz2[i][:], in0=raws["y", g, j // 2][:, j % 2, :], scalar=nf[:, i : i + 1], in1=raws["g", g][:, j, :], op0=ALU.mult, op1=ALU.mult)
+
+        def transposes(key, src):
+            bank = psum.tile([P, 2, 2, P], F32, tag="tr", bufs=2)
+            words = src.bitcast(F32)
+            for c in range(2):
+                for u in range(2):
+                    T.transpose(bank[:, c, u, :], words[:, 256 * c + u : 256 * c + 256 : 2], ident[:])
+            trb[key] = bank
+
+        def tr_out(eng, key, i):
+            pk = (key, i // 2)
+            if pk not in grp:
+                pair = mid.tile([P, 2, 2, 512], BF16, tag="grp", bufs=3, align_bytes=64)
+                grp[pk] = pair
+            dst = grp[pk][:, i % 2].bitcast(F32).rearrange("p c (r u) -> p c r u", u=2)
+            src = trb[key, i][:].rearrange("p c u r -> p c r u")
+            COPY(eng)(out=dst, in_=src)
+
+        def B(i):
+            transposes(("d2", i), dz2[i][:])
+
+        def C(eng, i):
+            tr_out(eng, "d2", i)
+
+        def quant_pair(key, i, store, tag):
+            cs = mid.tile([P, 2, 2, P], U32, tag=tag, bufs=3, align_bytes=64)
+            sc = mid.tile([P, 2, 2, P], U8, tag=tag + "s", bufs=3, align_bytes=64)
+            V.quantize_mx(
+                out=cs[:].rearrange("p j c r -> p (j c r)").bitcast(E5M2),
+                scales=sc[:].rearrange("p j c r -> p (j c r)"),
+                in_=grp[key, i // 2][:].rearrange("p j c w -> p (j c w)"),
+            )
+            store[i // 2] = (cs, sc)
+
+        def Q(i):
+            quant_pair("d2", i, codes2, "c2")
+
+        def mm(out, ls, lc, rs, start, stop):
+            T.matmul_mx(out=out, lhsT=ls[0].bitcast(lc), lhsT_scale=ls[1], rhs=rs[0].bitcast(E4M3), rhs_scale=rs[1], start=start, stop=stop)
+
+        def bank_mm():
+            bank = psum.tile([P, 512], F32, tag="mm", bufs=6)
+            return bank
+
+        def E(i):
+            cs, sc = codes2[i // 2]
+            for n in range(2):
+                bank = bank_mm()
+                cols = slice(512 * n, 512 * n + 512)
+                for c in range(2):
+                    mm(bank[:], (cs[:, i % 2, c, :], sc[:, i % 2, c, :]), E5M2, (w4_codes[:, c, cols], w4_scales[:, c, cols]), c == 0, c == 1)
+                dhb[i, n] = bank
+
+        def SQ(i):
+            g, j = divmod(i, 4)
+            t = raws["h3", g, j // 2][:, j % 2, :]
+            S.activation(out=t, in_=t, func=ACT.Square)
+
+        def F(i):
+            g, j = divmod(i, 4)
+            if g not in dz1:
+                tokens = mid.tile([P, 4, 1024], BF16, tag="dz1", bufs=2, align_bytes=64)
+                dz1[g] = tokens
+            for n in range(2):
+                cols = slice(512 * n, 512 * n + 512)
+                V.scalar_tensor_tensor(out=dz1[g][:, j, cols], in0=raws["h3", g, j // 2][:, j % 2, cols], scalar=1.0, in1=dhb[i, n][:], op0=ALU.subtract, op1=ALU.mult)
+
+        def G(i):
+            g, j = divmod(i, 4)
+            transposes(("d1", i), dz1[g][:, j, :])
+
+        def H(eng, i):
+            tr_out(eng, "d1", i)
+
+        def I(i):
+            quant_pair("d1", i, codes1, "c1")
+
+        srcs = {"w4": (w4_codes, w4_scales), "w3": (w3_codes, w3_scales), "h2": (h2_codes, h2_scales), "t1": (t1_codes, t1_scales)}
+
+        def IL(eng, name, c, n):
+            t = mid.tile([P, 512, 4], BF16, tag="wg", bufs=4, align_bytes=64)
+            wg[name, c, n] = t
+            if name == "t1":
+                src = dz1[c][:, :, 512 * n : 512 * n + 512]
+            else:
+                src = raws[name, c, n // 2][:, :, 512 * (n % 2) : 512 * (n % 2) + 512]
+            COPY(eng)(out=t[:], in_=src.rearrange("p j w -> p w j"))
+
+        def QW(name, c, n):
+            cs, sc = srcs[name]
+            cols = slice(512 * n, 512 * n + 512)
+            V.quantize_mx(out=cs[:, c, cols].bitcast(E5M2 if name == "t1" else E4M3), scales=sc[:, c, cols], in_=wg[name, c, n][:].rearrange("p w j -> p (w j)"))
+
+        obank = {}
+
+        def J(i, ns=range(4)):
+            cs, sc = codes1[i // 2]
+            for n in ns:
+                bank = bank_mm()
+                obank[0, i, n] = bank
+                cols = slice(512 * n, 512 * n + 512)
+                for c in range(2):
+                    mm(bank[:], (cs[:, i % 2, c, :], sc[:, i % 2, c, :]), E5M2, (w3_codes[:, c, cols], w3_scales[:, c, cols]), c == 0, c == 1)
+
+        def J1(m, ns=range(4)):
+            rows = slice(P * m, P * m + P)
+            for n in ns:
+                bank = bank_mm()
+                obank[1, m, n] = bank
+                cols = slice(512 * n, 512 * n + 512)
+                for c in range(2):
+                    mm(bank[:], (t1_codes[:, c, rows], t1_scales[:, c, rows]), E5M2, (h2_codes[:, c, cols], h2_scales[:, c, cols]), c == 0, c == 1)
+
+        def K(o, i, n, eng):
+            if (o, i) not in stg:
+                result = raw.tile([P, 2048], F32, tag="raw", align_bytes=64)
+                stg[o, i] = result
+            COPY(eng)(out=stg[o, i][:, 512 * n : 512 * n + 512], in_=obank[o, i, n][:])
+
+        def ST(o, i, cols=slice(0, 2048)):
+            dst = o0_v[i // 4, :, i % 4, cols] if o == 0 else out_1[P * i : P * i + P, cols]
+            nc.sync.dma_start(out=dst, in_=stg[o, i][:, cols])
+
+
+        A(0); B(0); A(1); B(1)
+        C("s", 0); C("v", 1)
+        IL("v", "w4", 0, 0)
+        Q(0)
+        IL("s", "w4", 0, 1)
+        QW("w4", 0, 0)
+        A(2); B(2); A(3); B(3)
+        IL("v", "w4", 1, 0)
+        C("s", 2); C("s", 3)
+        IL("v", "w4", 1, 1)
+        QW("w4", 0, 1); QW("w4", 1, 0); Q(2); QW("w4", 1, 1)
+        SQ(0); SQ(1)
+        E(0); E(1)
+        load_tok("y", y_v, 1, 1, BOTH); load_tok("h3", h3_v, 1, 0, BOTH)
+        F(0); G(0); F(1); G(1)
+        IL("s", "w3", 0, 0)
+        E(2)
+        H("s", 0); H("s", 1)
+        IL("v", "w3", 1, 0)
+        I(0); SQ(2); SQ(3); E(3)
+        QW("w3", 0, 0); QW("w3", 1, 0)
+        IL("v", "w3", 0, 1); IL("s", "w3", 1, 1); QW("w3", 0, 1); QW("w3", 1, 1)
+        F(2); G(2); F(3); G(3)
+        J(0, [0, 1]); J(1, [0, 1])
+        load_tok("h3", h3_v, 1, 1, BOTH); load_w("h2", h2_v, 0, 0); load_w("h2", h2_v, 1, 0)
+        H("s", 2); H("s", 3); I(2)
+        K(0, 0, 0, "s"); K(0, 0, 1, "s"); K(0, 1, 0, "s"); K(0, 1, 1, "s")
+        IL("v", "w3", 0, 2); IL("s", "w3", 1, 2); QW("w3", 0, 2); QW("w3", 1, 2)
+        IL("v", "w3", 0, 3); IL("v", "w3", 1, 3); QW("w3", 0, 3); QW("w3", 1, 3)
+        load_w("h2", h2_v, 0, 1); load_w("h2", h2_v, 1, 1)
+        J(0, [2, 3]); K(0, 0, 2, "s"); K(0, 0, 3, "s"); ST(0, 0)
+        J(1, [2, 3]); K(0, 1, 2, "s"); K(0, 1, 3, "v"); ST(0, 1)
+        A(4); B(4); C("s", 4); A(5); B(5); C("s", 5)
+        for i in (2, 3):
+            J(i)
+            K(0, i, 0, "s"); K(0, i, 1, "s"); K(0, i, 2, "v"); K(0, i, 3, "s"); ST(0, i)
+        A(6); B(6); A(7); B(7); Q(4); C("s", 6); C("s", 7); SQ(4); E(4); SQ(5); E(5); Q(6)
+        F(4); G(4); F(5); G(5); SQ(6); SQ(7); E(6); E(7)
+        H("s", 4); H("s", 5); I(4); F(6); G(6); F(7); G(7)
+        for i in (4, 5):
+            J(i); K(0, i, 0, "s"); K(0, i, 1, "s"); K(0, i, 2, "v"); K(0, i, 3, "s"); ST(0, i)
+        H("s", 6); H("v", 7); I(6)
+        IL("v", "t1", 0, 0); IL("v", "t1", 0, 1); QW("t1", 0, 0); QW("t1", 0, 1)
+        for i in (6, 7):
+            J(i); K(0, i, 0, "s"); K(0, i, 1, "s"); K(0, i, 2, "v"); K(0, i, 3, "s"); ST(0, i)
+        IL("v", "t1", 1, 0); IL("s", "t1", 1, 1); QW("t1", 1, 0); QW("t1", 1, 1)
+        IL("v", "h2", 0, 0); IL("v", "h2", 1, 0); QW("h2", 0, 0); QW("h2", 1, 0)
+        IL("v", "h2", 0, 1); IL("s", "h2", 1, 1); QW("h2", 0, 1); QW("h2", 1, 1)
+        for m in range(4):
+            J1(m, [0, 1])
+            K(1, m, 0, "s"); K(1, m, 1, "s"); ST(1, m, slice(0, 1024))
+        IL("v", "h2", 0, 2); IL("v", "h2", 1, 2); QW("h2", 0, 2); QW("h2", 1, 2)
+        IL("s", "h2", 0, 3); IL("v", "h2", 1, 3); QW("h2", 0, 3); QW("h2", 1, 3)
+        for m in range(4):
+            J1(m, [2, 3])
+            K(1, m, 2, "v"); K(1, m, 3, "s"); ST(1, m, slice(1024, 2048))
+        for m in range(4, 8):
+            J1(m)
+            for n in range(4):
+                K(1, m, n, "vs"[n % 2])
+            if m < 7:
+                ST(1, m)
+            else:
+                ST(1, m, slice(0, 1024)); ST(1, m, slice(1024, 2048))

@@ -3,8 +3,17 @@ from contextlib import ExitStack
 import concourse.mybir as mybir
 from concourse.masks import make_identity
 
-FLOPS = 2 * 1024 * 1024 * 1024 + 2 * 2 * 1024 * 1024 * 2048
-BYTES = 2 * (1024 * 2048 * 2 + 1024 * 1024 * 2 + 2 * 1024) + 2 * 4 * 1024 * 1024 + 2 * 4 * 1024 * 2048
+TOKENS = 1024
+OUTS = 1024
+HIDDEN = 1024
+INS = 2048
+
+FLOPS = 2 * TOKENS * OUTS * HIDDEN + 2 * 2 * TOKENS * HIDDEN * INS
+BYTES = (
+    2 * (TOKENS * INS + HIDDEN * INS + OUTS * HIDDEN + TOKENS * OUTS + 2 * TOKENS)
+    + 4 * (TOKENS * OUTS + TOKENS * HIDDEN)
+    + 4 * (TOKENS * INS + HIDDEN * INS)
+)
 
 F32 = mybir.dt.float32
 BF16 = mybir.dt.bfloat16
@@ -16,292 +25,469 @@ ALU = mybir.AluOpType
 ACT = mybir.ActivationFunctionType
 
 P = 128
+PACK = 4
+BANK = 512
+PASSES = 2
 
 
 def tile_mlp_v1_pa_v_kernel(tc, h2, W3, b3, W4, b4, x0, x1, h3, y, grad_out, out_0, out_1):
     nc = tc.nc
-    V, S, T = nc.vector, nc.scalar, nc.tensor
-    y_v = y.rearrange("(g p j) d -> g p j d", p=P, j=4)
-    g_v = grad_out.rearrange("(g p j) d -> g p j d", p=P, j=4)
-    h3_v = h3.rearrange("(g p j) d -> g p j d", p=P, j=4)
-    W4_v = W4.rearrange("(c p j) f -> c p j f", p=P, j=4)
-    W3_v = W3.rearrange("(c p j) f -> c p j f", p=P, j=4)
-    h2_v = h2.rearrange("(c p j) f -> c p j f", p=P, j=4)
-    o0_v = out_0.rearrange("(g p j) f -> g p j f", p=P, j=4)
+    vector, scalar, tensor = nc.vector, nc.scalar, nc.tensor
+
+    y_view, grad_view, h3_view, out_0_view = [
+        a.rearrange("(g p j) d -> g p j d", p=P, j=PACK) for a in (y, grad_out, h3, out_0)
+    ]
+    weight_view = {
+        name: a.rearrange("(c p t) f -> c p t f", p=P, t=PACK) for name, a in (("W4", W4), ("W3", W3), ("h2", h2))
+    }
 
     with ExitStack() as ctx:
         keep = ctx.enter_context(tc.tile_pool(name="keep", bufs=1))
-        raw = ctx.enter_context(tc.tile_pool(name="raw", bufs=13))
-        mid = ctx.enter_context(tc.tile_pool(name="mid", bufs=3))
+        ring = ctx.enter_context(tc.tile_pool(name="ring", bufs=1))
         psum = ctx.enter_context(tc.psum_pool(name="psum", bufs=1))
+        ctx.enter_context(tc.manual_schedule())
 
-        w4_codes = keep.tile([P, 2, 1024], U32, align_bytes=64)
-        w4_scales = keep.tile([P, 2, 1024], U8, align_bytes=64)
-        w3_codes = keep.tile([P, 2, 2048], U32, align_bytes=64)
-        w3_scales = keep.tile([P, 2, 2048], U8, align_bytes=64)
-        h2_codes = keep.tile([P, 2, 2048], U32, align_bytes=64)
-        h2_scales = keep.tile([P, 2, 2048], U8, align_bytes=64)
-        t1_codes = keep.tile([P, 2, 1024], U32, align_bytes=64)
-        t1_scales = keep.tile([P, 2, 1024], U8, align_bytes=64)
-        ident = keep.tile([P, P], F32)
-        make_identity(nc, ident[:])
+        codes, scales = {}, {}
+        for name, width in (("W4", HIDDEN), ("W3", INS), ("h2", INS), ("dz1", HIDDEN)):
+            operand_codes = keep.tile([P, PASSES, width], U32, tag="codes " + name, align_bytes=64)
+            operand_scales = keep.tile([P, PASSES, width], U8, tag="scales " + name, align_bytes=64)
+            codes[name], scales[name] = operand_codes, operand_scales
 
-        def COPY(eng):
-            return V.tensor_copy if eng == "v" else S.copy
+        identity = keep.tile([P, P], F32)
+        make_identity(nc, identity[:])
 
-        raws = {}
+        x0_sb = keep.tile([P, 2, PACK], BF16)
+        x1_sb = keep.tile([P, 2, PACK], BF16)
+        scalar.dma_start(out=x0_sb[:], in_=x0.rearrange("(g p j) -> p g j", p=P, j=PACK))
+        scalar.dma_start(out=x1_sb[:], in_=x1.rearrange("(g p j) -> p g j", p=P, j=PACK))
 
-        def new_raw(name, shape, dtype):
-            chunk = raw.tile(shape, dtype, tag="raw", align_bytes=64)
-            raws[name] = chunk
-            return chunk
-
-        def load_g(g, js):
-            if ("g", g) not in raws:
-                new_raw(("g", g), [P, 4, 1024], BF16)
-            nc.sync.dma_start(out=raws["g", g][:, js, :], in_=g_v[g, :, js, :])
-
-        def load_tok(name, view, g, half, js):
-            key = (name, g, half)
-            if key not in raws:
-                new_raw(key, [P, 2, 1024], F32)
-            nc.sync.dma_start(out=raws[key][:, js, :], in_=view[g, :, slice(2 * half + js.start, 2 * half + js.stop), :])
-
-        def load_w(name, view, c, half):
-            t = new_raw((name, c, half), [P, 4, 1024], BF16)
-            nc.sync.dma_start(out=t[:], in_=view[c, :, :, 1024 * half : 1024 * half + 1024])
-
-        BOTH = slice(0, 2)
-        x0_sb = keep.tile([P, 2, 4], BF16)
-        x1_sb = keep.tile([P, 2, 4], BF16)
-        nc.scalar.dma_start(out=x0_sb[:], in_=x0.rearrange("(g p j) -> p g j", p=P, j=4))
-        nc.scalar.dma_start(out=x1_sb[:], in_=x1.rearrange("(g p j) -> p g j", p=P, j=4))
         warm = keep.tile([P, 2], F32)
-        V.memset(warm[:], 0.0)
-        S.activation(out=warm[:, 1:2], in_=warm[:, 0:1], func=ACT.Square)
+        vector.memset(warm[:], 0.0)
+        scalar.activation(out=warm[:, 1:2], in_=warm[:, 0:1], func=ACT.Square)
 
-        load_g(0, slice(0, 2))
-        load_tok("y", y_v, 0, 0, slice(0, 1))
-        load_tok("y", y_v, 0, 0, slice(1, 2))
-        load_w("w4", W4_v, 0, 0)
-        load_g(0, slice(2, 4))
-        load_tok("y", y_v, 0, 1, BOTH)
-        load_w("w4", W4_v, 1, 0)
-        load_tok("h3", h3_v, 0, 0, BOTH)
-        load_tok("h3", h3_v, 0, 1, BOTH)
-        for half in range(2):
-            for c in range(2):
-                load_w("w3", W3_v, c, half)
-        load_g(1, slice(0, 4))
-        load_tok("y", y_v, 1, 0, BOTH)
+        x0_row = x0_sb[:].rearrange("p g j -> p (g j)")
+        x1_row = x1_sb[:].rearrange("p g j -> p (g j)")
+        rows = keep.tile([P, 7, 2 * PACK], F32)
+        safe, inverse, low, low_part, high, high_part, factor = [rows[:, r, :] for r in range(7)]
+        vector.tensor_scalar(out=safe, in0=x1_row, scalar1=2.0**-126, scalar2=None, op0=ALU.max)
+        vector.scalar_tensor_tensor(out=high, in0=x1_row, scalar=2.0, in1=x0_row, op0=ALU.mult, op1=ALU.subtract)
+        vector.scalar_tensor_tensor(out=low, in0=x1_row, scalar=-0.5, in1=x0_row, op0=ALU.mult, op1=ALU.add)
+        vector.reciprocal(out=inverse, in_=safe)
+        vector.scalar_tensor_tensor(out=high_part, in0=high, scalar=0.0, in1=inverse, op0=ALU.max, op1=ALU.mult)
+        vector.scalar_tensor_tensor(out=low_part, in0=low, scalar=0.0, in1=inverse, op0=ALU.max, op1=ALU.mult)
+        vector.tensor_scalar(out=high_part, in0=high_part, scalar1=1.5, scalar2=-8.0, op0=ALU.min, op1=ALU.mult)
+        vector.scalar_tensor_tensor(out=factor, in0=low_part, scalar=1.5, in1=high_part, op0=ALU.min, op1=ALU.mult)
 
-        xa = x0_sb[:].rearrange("p g j -> p (g j)")
-        xb = x1_sb[:].rearrange("p g j -> p (g j)")
-        lim = keep.tile([P, 8, 8], F32)
-        npos, safe, inv, a, a2, b, b2, nf = [lim[:, i, :] for i in range(8)]
-        V.tensor_scalar(out=npos, in0=xb, scalar1=0.0, scalar2=None, op0=ALU.is_le)
-        V.scalar_tensor_tensor(out=a, in0=xb, scalar=-0.5, in1=xa, op0=ALU.mult, op1=ALU.add)
-        V.scalar_tensor_tensor(out=safe, in0=xb, scalar=0.0, in1=npos, op0=ALU.max, op1=ALU.add)
-        V.scalar_tensor_tensor(out=b, in0=xb, scalar=2.0, in1=xa, op0=ALU.mult, op1=ALU.subtract)
-        V.reciprocal(out=inv, in_=safe)
-        V.scalar_tensor_tensor(out=b2, in0=b, scalar=0.0, in1=inv, op0=ALU.max, op1=ALU.mult)
-        V.scalar_tensor_tensor(out=a2, in0=a, scalar=0.0, in1=inv, op0=ALU.max, op1=ALU.mult)
-        V.tensor_scalar(out=b2, in0=b2, scalar1=1.5, scalar2=-8.0, op0=ALU.min, op1=ALU.mult)
-        V.scalar_tensor_tensor(out=nf, in0=a2, scalar=1.5, in1=b2, op0=ALU.min, op1=ALU.mult)
+        raw = {}
+        dz2_rows, dz1_rows = {}, {}
+        turned = {}
+        features = {}
+        stationary = {}
+        grouped = {}
+        banks = {}
+        results = {}
 
-        dz2, dz1, grp, tok, codes2, codes1, stg, wg = {}, {}, {}, {}, {}, {}, {}, {}
-        trb, dhb = {}, {}
+        def copy_on(engine):
+            return vector.tensor_copy if engine == "v" else scalar.copy
 
-        def A(i):
-            g, j = divmod(i, 4)
-            rows = mid.tile([P, 1024], BF16, tag="dz2", bufs=3, align_bytes=64)
-            dz2[i] = rows
-            V.scalar_tensor_tensor(out=dz2[i][:], in0=raws["y", g, j // 2][:, j % 2, :], scalar=nf[:, i : i + 1], in1=raws["g", g][:, j, :], op0=ALU.mult, op1=ALU.mult)
 
-        def transposes(key, src):
-            bank = psum.tile([P, 2, 2, P], F32, tag="tr", bufs=2)
-            words = src.bitcast(F32)
-            for c in range(2):
-                for u in range(2):
-                    T.transpose(bank[:, c, u, :], words[:, 256 * c + u : 256 * c + 256 : 2], ident[:])
-            trb[key] = bank
+        def new_chunk(key, shape, dtype):
+            chunk = ring.tile(shape, dtype, tag="chunk", bufs=9, align_bytes=64)
+            raw[key] = chunk
 
-        def tr_out(eng, key, i):
-            pk = (key, i // 2)
-            if pk not in grp:
-                pair = mid.tile([P, 2, 2, 512], BF16, tag="grp", bufs=3, align_bytes=64)
-                grp[pk] = pair
-            dst = grp[pk][:, i % 2].bitcast(F32).rearrange("p c (r u) -> p c r u", u=2)
-            src = trb[key, i][:].rearrange("p c u r -> p c r u")
-            COPY(eng)(out=dst, in_=src)
+        def load_grad(g, first, last):
+            if ("grad", g) not in raw:
+                new_chunk(("grad", g), [P, PACK, OUTS], BF16)
+            nc.sync.dma_start(out=raw["grad", g][:, first:last, :], in_=grad_view[g, :, first:last, :])
 
-        def B(i):
-            transposes(("d2", i), dz2[i][:])
-
-        def C(eng, i):
-            tr_out(eng, "d2", i)
-
-        def quant_pair(key, i, store, tag):
-            cs = mid.tile([P, 2, 2, P], U32, tag=tag, bufs=3, align_bytes=64)
-            sc = mid.tile([P, 2, 2, P], U8, tag=tag + "s", bufs=3, align_bytes=64)
-            V.quantize_mx(
-                out=cs[:].rearrange("p j c r -> p (j c r)").bitcast(E5M2),
-                scales=sc[:].rearrange("p j c r -> p (j c r)"),
-                in_=grp[key, i // 2][:].rearrange("p j c w -> p (j c w)"),
+        def load_tokens(name, g, first, last):
+            view = y_view if name == "y" else h3_view
+            half = first // 2
+            if (name, g, half) not in raw:
+                new_chunk((name, g, half), [P, 2, OUTS], F32)
+            nc.sync.dma_start(
+                out=raw[name, g, half][:, first - 2 * half : last - 2 * half, :], in_=view[g, :, first:last, :]
             )
-            store[i // 2] = (cs, sc)
 
-        def Q(i):
-            quant_pair("d2", i, codes2, "c2")
-
-        def mm(out, ls, lc, rs, start, stop):
-            T.matmul_mx(out=out, lhsT=ls[0].bitcast(lc), lhsT_scale=ls[1], rhs=rs[0].bitcast(E4M3), rhs_scale=rs[1], start=start, stop=stop)
-
-        def bank_mm():
-            bank = psum.tile([P, 512], F32, tag="mm", bufs=6)
-            return bank
-
-        def E(i):
-            cs, sc = codes2[i // 2]
-            for n in range(2):
-                bank = bank_mm()
-                cols = slice(512 * n, 512 * n + 512)
-                for c in range(2):
-                    mm(bank[:], (cs[:, i % 2, c, :], sc[:, i % 2, c, :]), E5M2, (w4_codes[:, c, cols], w4_scales[:, c, cols]), c == 0, c == 1)
-                dhb[i, n] = bank
-
-        def SQ(i):
-            g, j = divmod(i, 4)
-            t = raws["h3", g, j // 2][:, j % 2, :]
-            S.activation(out=t, in_=t, func=ACT.Square)
-
-        def F(i):
-            g, j = divmod(i, 4)
-            if g not in dz1:
-                tokens = mid.tile([P, 4, 1024], BF16, tag="dz1", bufs=2, align_bytes=64)
-                dz1[g] = tokens
-            for n in range(2):
-                cols = slice(512 * n, 512 * n + 512)
-                V.scalar_tensor_tensor(out=dz1[g][:, j, cols], in0=raws["h3", g, j // 2][:, j % 2, cols], scalar=1.0, in1=dhb[i, n][:], op0=ALU.subtract, op1=ALU.mult)
-
-        def G(i):
-            g, j = divmod(i, 4)
-            transposes(("d1", i), dz1[g][:, j, :])
-
-        def H(eng, i):
-            tr_out(eng, "d1", i)
-
-        def I(i):
-            quant_pair("d1", i, codes1, "c1")
-
-        srcs = {"w4": (w4_codes, w4_scales), "w3": (w3_codes, w3_scales), "h2": (h2_codes, h2_scales), "t1": (t1_codes, t1_scales)}
-
-        def IL(eng, name, c, n):
-            t = mid.tile([P, 512, 4], BF16, tag="wg", bufs=4, align_bytes=64)
-            wg[name, c, n] = t
-            if name == "t1":
-                src = dz1[c][:, :, 512 * n : 512 * n + 512]
+        def load_weight(name, c):
+            if name == "W4":
+                new_chunk((name, c), [P, PACK, HIDDEN], BF16)
             else:
-                src = raws[name, c, n // 2][:, :, 512 * (n % 2) : 512 * (n % 2) + 512]
-            COPY(eng)(out=t[:], in_=src.rearrange("p j w -> p w j"))
-
-        def QW(name, c, n):
-            cs, sc = srcs[name]
-            cols = slice(512 * n, 512 * n + 512)
-            V.quantize_mx(out=cs[:, c, cols].bitcast(E5M2 if name == "t1" else E4M3), scales=sc[:, c, cols], in_=wg[name, c, n][:].rearrange("p w j -> p (w j)"))
-
-        obank = {}
-
-        def J(i, ns=range(4)):
-            cs, sc = codes1[i // 2]
-            for n in ns:
-                bank = bank_mm()
-                obank[0, i, n] = bank
-                cols = slice(512 * n, 512 * n + 512)
-                for c in range(2):
-                    mm(bank[:], (cs[:, i % 2, c, :], sc[:, i % 2, c, :]), E5M2, (w3_codes[:, c, cols], w3_scales[:, c, cols]), c == 0, c == 1)
-
-        def J1(m, ns=range(4)):
-            rows = slice(P * m, P * m + P)
-            for n in ns:
-                bank = bank_mm()
-                obank[1, m, n] = bank
-                cols = slice(512 * n, 512 * n + 512)
-                for c in range(2):
-                    mm(bank[:], (t1_codes[:, c, rows], t1_scales[:, c, rows]), E5M2, (h2_codes[:, c, cols], h2_scales[:, c, cols]), c == 0, c == 1)
-
-        def K(o, i, n, eng):
-            if (o, i) not in stg:
-                result = raw.tile([P, 2048], F32, tag="raw", align_bytes=64)
-                stg[o, i] = result
-            COPY(eng)(out=stg[o, i][:, 512 * n : 512 * n + 512], in_=obank[o, i, n][:])
-
-        def ST(o, i, cols=slice(0, 2048)):
-            dst = o0_v[i // 4, :, i % 4, cols] if o == 0 else out_1[P * i : P * i + P, cols]
-            nc.sync.dma_start(out=dst, in_=stg[o, i][:, cols])
+                whole = ring.tile([P, PACK, INS], BF16, tag="whole", bufs=2, align_bytes=64)
+                raw[name, c] = whole
+            nc.sync.dma_start(out=raw[name, c][:], in_=weight_view[name][c])
 
 
-        A(0); B(0); A(1); B(1)
-        C("s", 0); C("v", 1)
-        IL("v", "w4", 0, 0)
-        Q(0)
-        IL("s", "w4", 0, 1)
-        QW("w4", 0, 0)
-        A(2); B(2); A(3); B(3)
-        IL("v", "w4", 1, 0)
-        C("s", 2); C("s", 3)
-        IL("v", "w4", 1, 1)
-        QW("w4", 0, 1); QW("w4", 1, 0); Q(2); QW("w4", 1, 1)
-        SQ(0); SQ(1)
-        E(0); E(1)
-        load_tok("y", y_v, 1, 1, BOTH); load_tok("h3", h3_v, 1, 0, BOTH)
-        F(0); G(0); F(1); G(1)
-        IL("s", "w3", 0, 0)
-        E(2)
-        H("s", 0); H("s", 1)
-        IL("v", "w3", 1, 0)
-        I(0); SQ(2); SQ(3); E(3)
-        QW("w3", 0, 0); QW("w3", 1, 0)
-        IL("v", "w3", 0, 1); IL("s", "w3", 1, 1); QW("w3", 0, 1); QW("w3", 1, 1)
-        F(2); G(2); F(3); G(3)
-        J(0, [0, 1]); J(1, [0, 1])
-        load_tok("h3", h3_v, 1, 1, BOTH); load_w("h2", h2_v, 0, 0); load_w("h2", h2_v, 1, 0)
-        H("s", 2); H("s", 3); I(2)
-        K(0, 0, 0, "s"); K(0, 0, 1, "s"); K(0, 1, 0, "s"); K(0, 1, 1, "s")
-        IL("v", "w3", 0, 2); IL("s", "w3", 1, 2); QW("w3", 0, 2); QW("w3", 1, 2)
-        IL("v", "w3", 0, 3); IL("v", "w3", 1, 3); QW("w3", 0, 3); QW("w3", 1, 3)
-        load_w("h2", h2_v, 0, 1); load_w("h2", h2_v, 1, 1)
-        J(0, [2, 3]); K(0, 0, 2, "s"); K(0, 0, 3, "s"); ST(0, 0)
-        J(1, [2, 3]); K(0, 1, 2, "s"); K(0, 1, 3, "v"); ST(0, 1)
-        A(4); B(4); C("s", 4); A(5); B(5); C("s", 5)
-        for i in (2, 3):
-            J(i)
-            K(0, i, 0, "s"); K(0, i, 1, "s"); K(0, i, 2, "v"); K(0, i, 3, "s"); ST(0, i)
-        A(6); B(6); A(7); B(7); Q(4); C("s", 6); C("s", 7); SQ(4); E(4); SQ(5); E(5); Q(6)
-        F(4); G(4); F(5); G(5); SQ(6); SQ(7); E(6); E(7)
-        H("s", 4); H("s", 5); I(4); F(6); G(6); F(7); G(7)
-        for i in (4, 5):
-            J(i); K(0, i, 0, "s"); K(0, i, 1, "s"); K(0, i, 2, "v"); K(0, i, 3, "s"); ST(0, i)
-        H("s", 6); H("v", 7); I(6)
-        IL("v", "t1", 0, 0); IL("v", "t1", 0, 1); QW("t1", 0, 0); QW("t1", 0, 1)
-        for i in (6, 7):
-            J(i); K(0, i, 0, "s"); K(0, i, 1, "s"); K(0, i, 2, "v"); K(0, i, 3, "s"); ST(0, i)
-        IL("v", "t1", 1, 0); IL("s", "t1", 1, 1); QW("t1", 1, 0); QW("t1", 1, 1)
-        IL("v", "h2", 0, 0); IL("v", "h2", 1, 0); QW("h2", 0, 0); QW("h2", 1, 0)
-        IL("v", "h2", 0, 1); IL("s", "h2", 1, 1); QW("h2", 0, 1); QW("h2", 1, 1)
-        for m in range(4):
-            J1(m, [0, 1])
-            K(1, m, 0, "s"); K(1, m, 1, "s"); ST(1, m, slice(0, 1024))
-        IL("v", "h2", 0, 2); IL("v", "h2", 1, 2); QW("h2", 0, 2); QW("h2", 1, 2)
-        IL("s", "h2", 0, 3); IL("v", "h2", 1, 3); QW("h2", 0, 3); QW("h2", 1, 3)
-        for m in range(4):
-            J1(m, [2, 3])
-            K(1, m, 2, "v"); K(1, m, 3, "s"); ST(1, m, slice(1024, 2048))
-        for m in range(4, 8):
-            J1(m)
-            for n in range(4):
-                K(1, m, n, "vs"[n % 2])
-            if m < 7:
-                ST(1, m)
-            else:
-                ST(1, m, slice(0, 1024)); ST(1, m, slice(1024, 2048))
+        def interleave(name, c, n, engines):
+            for k, engine in enumerate(engines):
+                cols = slice(BANK * (n + k), BANK * (n + k + 1))
+                source = (dz1_rows[c] if name == "dz1" else raw[name, c])[:, :, cols]
+                words = ring.tile([P, BANK, PACK], BF16, tag="grouped", bufs=4, align_bytes=64)
+                grouped[name, c, n + k] = words
+                copy_on(engine)(
+                    out=words[:].rearrange("p (b i) t -> p b t i", i=4),
+                    in_=source.rearrange("p t (b i) -> p b t i", i=4),
+                )
+
+        def quantise(name, c, *numbers):
+            for n in numbers:
+                cols = slice(BANK * n, BANK * n + BANK)
+                vector.quantize_mx(
+                    out=codes[name][:, c, cols].bitcast(E5M2 if name == "dz1" else E4M3),
+                    scales=scales[name][:, c, cols],
+                    in_=grouped[name, c, n][:].rearrange("p w t -> p (w t)"),
+                )
+
+
+        def turn(name, i):
+            tile_rows = dz2_rows[i][:] if name == "dz2" else dz1_rows[i // PACK][:, i % PACK, :]
+            bank = psum.tile([P, PASSES, 2, P], F32, tag="turned", bufs=2)
+            words = tile_rows.bitcast(F32)
+            for c in range(PASSES):
+                for u in range(2):
+                    tensor.transpose(bank[:, c, u, :], words[:, 256 * c + u : 256 * c + 256 : 2], identity[:])
+            turned[name, i] = bank
+
+        def turn_out(name, i, engine):
+            if (name, i // 2) not in features:
+                pair = ring.tile([P, 2, PASSES, P * PACK], BF16, tag="features", bufs=3, align_bytes=64)
+                features[name, i // 2] = pair
+            copy_on(engine)(
+                out=features[name, i // 2][:, i % 2].bitcast(F32).rearrange("p c (r u) -> p c r u", u=2),
+                in_=turned[name, i][:].rearrange("p c u r -> p c r u"),
+            )
+
+        def quantise_pair(name, pair):
+            pair_codes = ring.tile([P, 2, PASSES, P], U32, tag="codes of " + name, bufs=3, align_bytes=64)
+            pair_scales = ring.tile([P, 2, PASSES, P], U8, tag="scales of " + name, bufs=3, align_bytes=64)
+            vector.quantize_mx(
+                out=pair_codes[:].rearrange("p i c r -> p (i c r)").bitcast(E5M2),
+                scales=pair_scales[:].rearrange("p i c r -> p (i c r)"),
+                in_=features[name, pair][:].rearrange("p i c w -> p (i c w)"),
+            )
+            stationary[name, pair] = (pair_codes, pair_scales)
+
+
+        def make_dz2(i):
+            g, j = divmod(i, PACK)
+            tile_rows = ring.tile([P, OUTS], BF16, tag="dz2", bufs=3, align_bytes=64)
+            dz2_rows[i] = tile_rows
+            vector.scalar_tensor_tensor(
+                out=tile_rows[:],
+                in0=raw["y", g, j // 2][:, j % 2, :],
+                scalar=factor[:, i : i + 1],
+                in1=raw["grad", g][:, j, :],
+                op0=ALU.mult,
+                op1=ALU.mult,
+            )
+
+        def square_h3(i):
+            g, j = divmod(i, PACK)
+            h3_rows = raw["h3", g, j // 2][:, j % 2, :]
+            scalar.activation(out=h3_rows, in_=h3_rows, func=ACT.Square)
+
+        def make_dz1(i, *halves):
+            g, j = divmod(i, PACK)
+            if g not in dz1_rows:
+                group_rows = ring.tile([P, PACK, HIDDEN], BF16, tag="dz1", bufs=2, align_bytes=64)
+                dz1_rows[g] = group_rows
+            for n in halves:
+                cols = slice(BANK * n, BANK * n + BANK)
+                vector.scalar_tensor_tensor(
+                    out=dz1_rows[g][:, j, cols],
+                    in0=raw["h3", g, j // 2][:, j % 2, cols],
+                    scalar=1.0,
+                    in1=banks["dh", i, n][:],
+                    op0=ALU.subtract,
+                    op1=ALU.mult,
+                )
+
+
+        def product(key, left_codes, left_scales, name, n):
+            cols = slice(BANK * n, BANK * n + BANK)
+            bank = psum.tile([P, BANK], F32, tag="sums", bufs=6)
+            banks[key] = bank
+            for c in range(PASSES):
+                tensor.matmul_mx(
+                    out=bank[:],
+                    lhsT=left_codes[:, c, :].bitcast(E5M2),
+                    lhsT_scale=left_scales[:, c, :],
+                    rhs=codes[name][:, c, cols].bitcast(E4M3),
+                    rhs_scale=scales[name][:, c, cols],
+                    start=(c == 0),
+                    stop=(c == PASSES - 1),
+                )
+
+        def tile_product(key, left, i, name, n):
+            pair_codes, pair_scales = stationary[left, i // 2]
+            product(key + (i, n), pair_codes[:, i % 2], pair_scales[:, i % 2], name, n)
+
+        def make_dh(i, *halves):
+            for n in halves:
+                tile_product(("dh",), "dz2", i, "W4", n)
+
+        def out0(i, *numbers):
+            for n in numbers:
+                tile_product(("out", 0), "dz1", i, "W3", n)
+
+        def out1(m, *numbers):
+            hidden = slice(P * m, P * m + P)
+            for n in numbers:
+                product(("out", 1, m, n), codes["dz1"][:, :, hidden], scales["dz1"][:, :, hidden], "h2", n)
+
+        def empty(output, i, n, engines):
+            if (output, i) not in results:
+                result = ring.tile([P, INS], F32, tag="chunk", bufs=9, align_bytes=64)
+                results[output, i] = result
+            for k, engine in enumerate(engines):
+                cols = slice(BANK * (n + k), BANK * (n + k + 1))
+                copy_on(engine)(out=results[output, i][:, cols], in_=banks["out", output, i, n + k][:])
+
+        def store0(i):
+            nc.sync.dma_start(out=out_0_view[i // PACK, :, i % PACK, :], in_=results[0, i][:])
+
+        def store1(m, part):
+            first, last = {"left": (0, INS // 2), "right": (INS // 2, INS), "whole": (0, INS)}[part]
+            nc.sync.dma_start(out=out_1[P * m : P * m + P, first:last], in_=results[1, m][:, first:last])
+
+        load_grad(0, 0, 1)
+        load_grad(0, 1, 2)
+        load_weight("W4", 0)
+        load_weight("W4", 1)
+        interleave("W4", 0, 1, "s")
+        interleave("W4", 1, 1, "v")
+        interleave("W4", 1, 0, "s")
+        interleave("W4", 0, 0, "s")
+        load_tokens("y", 0, 0, 1)
+        load_tokens("y", 0, 1, 2)
+        make_dz2(0)
+        make_dz2(1)
+        quantise("W4", 1, 1)
+        quantise("W4", 1, 0)
+        quantise("W4", 0, 1)
+        quantise("W4", 0, 0)
+        turn("dz2", 0)
+        turn("dz2", 1)
+        load_weight("W3", 0)
+        load_grad(0, 2, 4)
+        turn_out("dz2", 0, "s")
+        turn_out("dz2", 1, "s")
+        load_tokens("y", 0, 2, 4)
+        quantise_pair("dz2", 0)
+        interleave("W3", 0, 0, "vsvs")
+        make_dh(1, 0)
+        make_dh(0, 0, 1)
+        quantise("W3", 0, 0, 1)
+        make_dz2(2)
+        make_dz2(3)
+        quantise("W3", 0, 2, 3)
+        load_tokens("h3", 0, 0, 2)
+        square_h3(0)
+        square_h3(1)
+        make_dz1(0, 0, 1)
+        make_dz1(1, 0)
+        load_weight("W3", 1)
+        load_tokens("h3", 0, 2, 4)
+        turn("dz2", 2)
+        turn_out("dz2", 2, "s")
+        make_dh(1, 1)
+        turn("dz2", 3)
+        turn("dz1", 0)
+        turn_out("dz2", 3, "s")
+        make_dz1(1, 1)
+        quantise_pair("dz2", 1)
+        turn_out("dz1", 0, "s")
+        interleave("W3", 1, 1, "s")
+        interleave("W3", 1, 0, "v")
+        interleave("W3", 1, 2, "v")
+        turn("dz1", 1)
+        make_dh(2, 0, 1)
+        make_dh(3, 0, 1)
+        quantise("W3", 1, 0, 1)
+        turn_out("dz1", 1, "s")
+        square_h3(2)
+        square_h3(3)
+        quantise_pair("dz1", 0)
+        out0(0, 1)
+        out0(1, 1)
+        quantise("W3", 1, 2)
+        make_dz1(2, 0, 1)
+        make_dz1(3, 0, 1)
+        load_tokens("y", 1, 0, 2)
+        load_grad(1, 0, 4)
+        make_dz2(4)
+        make_dz2(5)
+        out0(1, 0)
+        turn("dz1", 2)
+        turn("dz1", 3)
+        interleave("W3", 1, 3, "s")
+        out0(0, 0)
+        out0(0, 2)
+        empty(0, 0, 1, "s")
+        turn_out("dz1", 2, "s")
+        load_tokens("y", 1, 2, 4)
+        empty(0, 1, 0, "s")
+        turn_out("dz1", 3, "s")
+        empty(0, 0, 0, "s")
+        empty(0, 0, 2, "s")
+        quantise_pair("dz1", 1)
+        turn("dz2", 4)
+        out0(1, 2)
+        quantise("W3", 1, 3)
+        make_dz2(6)
+        make_dz2(7)
+        load_tokens("h3", 1, 0, 2)
+        out0(0, 3)
+        turn("dz2", 5)
+        turn_out("dz2", 4, "s")
+        empty(0, 1, 1, "ss")
+        turn("dz2", 6)
+        out0(2, 0)
+        interleave("dz1", 0, 0, "v")
+        turn_out("dz2", 5, "s")
+        empty(0, 2, 0, "v")
+        empty(0, 0, 3, "s")
+        turn("dz2", 7)
+        out0(1, 3)
+        out0(3, 0)
+        out0(2, 1)
+        quantise_pair("dz2", 2)
+        make_dh(5, 0)
+        make_dh(4, 0, 1)
+        load_weight("h2", 0)
+        turn_out("dz2", 6, "s")
+        turn_out("dz2", 7, "v")
+        square_h3(4)
+        square_h3(5)
+        empty(0, 1, 3, "v")
+        empty(0, 3, 0, "s")
+        empty(0, 2, 1, "s")
+        quantise_pair("dz2", 3)
+        make_dz1(5, 0)
+        make_dz1(4, 0)
+        load_tokens("h3", 1, 2, 4)
+        out0(2, 2)
+        interleave("h2", 0, 1, "s")
+        empty(0, 2, 2, "s")
+        make_dh(7, 0)
+        square_h3(7)
+        out0(3, 1)
+        quantise("dz1", 0, 0)
+        empty(0, 3, 1, "s")
+        interleave("h2", 0, 0, "v")
+        make_dh(5, 1)
+        make_dz1(4, 1)
+        make_dz1(5, 1)
+        quantise("h2", 0, 0, 1)
+        load_weight("h2", 1)
+        store0(1)
+        store0(0)
+        out0(3, 2)
+        turn("dz1", 4)
+        turn("dz1", 5)
+        out0(2, 3)
+        out0(3, 3)
+        make_dz1(7, 0)
+        make_dh(6, 0)
+        make_dh(7, 1)
+        make_dh(6, 1)
+        square_h3(6)
+        turn_out("dz1", 4, "s")
+        turn_out("dz1", 5, "s")
+        empty(0, 2, 3, "s")
+        empty(0, 3, 2, "ss")
+        interleave("h2", 1, 0, "vs")
+        quantise_pair("dz1", 2)
+        out0(4, 0, 1, 2)
+        make_dz1(7, 1)
+        make_dz1(6, 0, 1)
+        out0(5, 0, 1)
+        out0(4, 3)
+        empty(0, 4, 0, "ssss")
+        empty(0, 5, 0, "s")
+        interleave("dz1", 1, 0, "v")
+        quantise("h2", 1, 0, 1)
+        store0(2)
+        store0(3)
+        store0(4)
+        out0(5, 2)
+        turn("dz1", 6)
+        turn("dz1", 7)
+        empty(0, 5, 1, "ss")
+        interleave("h2", 0, 2, "v")
+        quantise("dz1", 1, 0)
+        interleave("h2", 0, 3, "v")
+        interleave("h2", 1, 2, "v")
+        out0(5, 3)
+        out1(0, 0)
+        out1(1, 0)
+        out1(0, 1)
+        out1(1, 1)
+        out1(2, 0)
+        empty(0, 5, 3, "s")
+        empty(1, 0, 0, "sv")
+        empty(1, 1, 0, "sv")
+        out1(3, 0, 1)
+        out1(2, 1)
+        quantise("h2", 0, 2)
+        quantise("h2", 1, 2)
+        quantise("h2", 0, 3)
+        out1(0, 2)
+        out1(1, 2)
+        interleave("h2", 1, 3, "s")
+        empty(1, 2, 0, "ss")
+        empty(1, 3, 0, "ss")
+        store0(5)
+        store1(0, "left")
+        store1(1, "left")
+        store1(2, "left")
+        store1(3, "left")
+        quantise("h2", 1, 3)
+        out1(0, 3)
+        out1(1, 3)
+        out1(2, 2, 3)
+        empty(1, 0, 2, "ss")
+        empty(1, 1, 2, "ss")
+        empty(1, 2, 3, "s")
+        interleave("dz1", 0, 1, "v")
+        interleave("dz1", 1, 1, "v")
+        quantise("dz1", 0, 1)
+        quantise("dz1", 1, 1)
+        out1(3, 2, 3)
+        out1(4, 0, 1)
+        empty(1, 2, 2, "v")
+        empty(1, 3, 2, "sv")
+        empty(1, 4, 0, "sv")
+        out1(4, 2, 3)
+        out1(5, 0, 1, 2, 3)
+        store1(0, "right")
+        store1(1, "right")
+        store1(2, "right")
+        store1(3, "right")
+        turn_out("dz1", 7, "s")
+        empty(1, 4, 2, "vs")
+        empty(1, 5, 0, "ss")
+        empty(1, 5, 3, "s")
+        out1(6, 0, 1, 2, 3)
+        turn_out("dz1", 6, "v")
+        quantise_pair("dz1", 3)
+        empty(1, 6, 0, "s")
+        empty(1, 5, 2, "v")
+        empty(1, 6, 1, "vvs")
+        out0(7, 0, 1, 2, 3)
+        empty(0, 7, 0, "vvvs")
+        store1(4, "whole")
+        store1(5, "whole")
+        store1(6, "whole")
+        store0(7)
+        out1(7, 0, 1)
+        out0(6, 0, 1, 2, 3)
+        empty(1, 7, 1, "s")
+        empty(0, 6, 0, "v")
+        empty(1, 7, 0, "v")
+        empty(0, 6, 1, "ssv")
+        out1(7, 2, 3)
+        store1(7, "left")
+        store0(6)
+        empty(1, 7, 2, "ss")
+        store1(7, "right")

@@ -10,7 +10,8 @@ INS = 2048
 
 FLOPS = 2 * TOKENS * OUTS * HIDDEN + 2 * 2 * TOKENS * HIDDEN * INS
 BYTES = (
-    2 * (TOKENS * INS + HIDDEN * INS + OUTS * HIDDEN + TOKENS * OUTS + 2 * TOKENS)
+    2 * (TOKENS * INS + HIDDEN * INS + OUTS * HIDDEN)
+    + 2 * (TOKENS * OUTS + 2 * TOKENS)
     + 4 * (TOKENS * OUTS + TOKENS * HIDDEN)
     + 4 * (TOKENS * INS + HIDDEN * INS)
 )
@@ -28,6 +29,16 @@ P = 128
 PACK = 4
 BANK = 512
 PASSES = 2
+PASS_WORDS = 256
+RUN = 8
+
+CHUNK_BUFS = 9
+WHOLE_BUFS = 2
+GROUPED_BUFS = 4
+TILE_BUFS = 3
+GROUP_BUFS = 2
+TURNED_BANKS = 2
+SUM_BANKS = 6
 
 
 def tile_mlp_v1_pa_v_kernel(tc, h2, W3, b3, W4, b4, x0, x1, h3, y, grad_out, out_0, out_1):
@@ -48,7 +59,7 @@ def tile_mlp_v1_pa_v_kernel(tc, h2, W3, b3, W4, b4, x0, x1, h3, y, grad_out, out
         ctx.enter_context(tc.manual_schedule())
 
         codes, scales = {}, {}
-        for name, width in (("W4", HIDDEN), ("W3", INS), ("h2", INS), ("dz1", HIDDEN)):
+        for name, width in (("W4", HIDDEN), ("W3", INS), ("h2", INS), ("dz1T", HIDDEN)):
             operand_codes = keep.tile([P, PASSES, width], U32, tag="codes " + name, align_bytes=64)
             operand_scales = keep.tile([P, PASSES, width], U8, tag="scales " + name, align_bytes=64)
             codes[name], scales[name] = operand_codes, operand_scales
@@ -67,8 +78,8 @@ def tile_mlp_v1_pa_v_kernel(tc, h2, W3, b3, W4, b4, x0, x1, h3, y, grad_out, out
 
         x0_row = x0_sb[:].rearrange("p g j -> p (g j)")
         x1_row = x1_sb[:].rearrange("p g j -> p (g j)")
-        rows = keep.tile([P, 7, 2 * PACK], F32)
-        safe, inverse, low, low_part, high, high_part, factor = [rows[:, r, :] for r in range(7)]
+        row_values = keep.tile([P, 7, 2 * PACK], F32)
+        safe, inverse, low, low_part, high, high_part, factor = [row_values[:, r, :] for r in range(7)]
         vector.tensor_scalar(out=safe, in0=x1_row, scalar1=2.0**-126, scalar2=None, op0=ALU.max)
         vector.scalar_tensor_tensor(out=high, in0=x1_row, scalar=2.0, in1=x0_row, op0=ALU.mult, op1=ALU.subtract)
         vector.scalar_tensor_tensor(out=low, in0=x1_row, scalar=-0.5, in1=x0_row, op0=ALU.mult, op1=ALU.add)
@@ -92,7 +103,7 @@ def tile_mlp_v1_pa_v_kernel(tc, h2, W3, b3, W4, b4, x0, x1, h3, y, grad_out, out
 
 
         def new_chunk(key, shape, dtype):
-            chunk = ring.tile(shape, dtype, tag="chunk", bufs=9, align_bytes=64)
+            chunk = ring.tile(shape, dtype, tag="chunk", bufs=CHUNK_BUFS, align_bytes=64)
             raw[key] = chunk
 
         def load_grad(g, first, last):
@@ -113,7 +124,7 @@ def tile_mlp_v1_pa_v_kernel(tc, h2, W3, b3, W4, b4, x0, x1, h3, y, grad_out, out
             if name == "W4":
                 new_chunk((name, c), [P, PACK, HIDDEN], BF16)
             else:
-                whole = ring.tile([P, PACK, INS], BF16, tag="whole", bufs=2, align_bytes=64)
+                whole = ring.tile([P, PACK, INS], BF16, tag="whole", bufs=WHOLE_BUFS, align_bytes=64)
                 raw[name, c] = whole
             nc.sync.dma_start(out=raw[name, c][:], in_=weight_view[name][c])
 
@@ -121,45 +132,46 @@ def tile_mlp_v1_pa_v_kernel(tc, h2, W3, b3, W4, b4, x0, x1, h3, y, grad_out, out
         def interleave(name, c, n, engines):
             for k, engine in enumerate(engines):
                 cols = slice(BANK * (n + k), BANK * (n + k + 1))
-                source = (dz1_rows[c] if name == "dz1" else raw[name, c])[:, :, cols]
-                words = ring.tile([P, BANK, PACK], BF16, tag="grouped", bufs=4, align_bytes=64)
-                grouped[name, c, n + k] = words
+                source = (dz1_rows[c] if name == "dz1T" else raw[name, c])[:, :, cols]
+                columns = ring.tile([P, BANK, PACK], BF16, tag="grouped", bufs=GROUPED_BUFS, align_bytes=64)
+                grouped[name, c, n + k] = columns
                 copy_on(engine)(
-                    out=words[:].rearrange("p (b i) t -> p b t i", i=4),
-                    in_=source.rearrange("p t (b i) -> p b t i", i=4),
+                    out=columns[:].rearrange("p (b i) t -> p b t i", i=RUN),
+                    in_=source.rearrange("p t (b i) -> p b t i", i=RUN),
                 )
 
         def quantise(name, c, *numbers):
             for n in numbers:
                 cols = slice(BANK * n, BANK * n + BANK)
                 vector.quantize_mx(
-                    out=codes[name][:, c, cols].bitcast(E5M2 if name == "dz1" else E4M3),
+                    out=codes[name][:, c, cols].bitcast(E5M2 if name == "dz1T" else E4M3),
                     scales=scales[name][:, c, cols],
-                    in_=grouped[name, c, n][:].rearrange("p w t -> p (w t)"),
+                    in_=grouped[name, c, n][:].rearrange("p f t -> p (f t)"),
                 )
 
 
         def turn(name, i):
             tile_rows = dz2_rows[i][:] if name == "dz2" else dz1_rows[i // PACK][:, i % PACK, :]
-            bank = psum.tile([P, PASSES, 2, P], F32, tag="turned", bufs=2)
+            bank = psum.tile([P, PASSES, 2, P], F32, tag="turned", bufs=TURNED_BANKS)
             words = tile_rows.bitcast(F32)
             for c in range(PASSES):
                 for u in range(2):
-                    tensor.transpose(bank[:, c, u, :], words[:, 256 * c + u : 256 * c + 256 : 2], identity[:])
+                    every_second = slice(PASS_WORDS * c + u, PASS_WORDS * (c + 1), 2)
+                    tensor.transpose(bank[:, c, u, :], words[:, every_second], identity[:])
             turned[name, i] = bank
 
         def turn_out(name, i, engine):
             if (name, i // 2) not in features:
-                pair = ring.tile([P, 2, PASSES, P * PACK], BF16, tag="features", bufs=3, align_bytes=64)
-                features[name, i // 2] = pair
+                pair_values = ring.tile([P, 2, PASSES, P * PACK], BF16, tag="features", bufs=TILE_BUFS, align_bytes=64)
+                features[name, i // 2] = pair_values
             copy_on(engine)(
                 out=features[name, i // 2][:, i % 2].bitcast(F32).rearrange("p c (r u) -> p c r u", u=2),
                 in_=turned[name, i][:].rearrange("p c u r -> p c r u"),
             )
 
         def quantise_pair(name, pair):
-            pair_codes = ring.tile([P, 2, PASSES, P], U32, tag="codes of " + name, bufs=3, align_bytes=64)
-            pair_scales = ring.tile([P, 2, PASSES, P], U8, tag="scales of " + name, bufs=3, align_bytes=64)
+            pair_codes = ring.tile([P, 2, PASSES, P], U32, tag="codes of " + name, bufs=TILE_BUFS, align_bytes=64)
+            pair_scales = ring.tile([P, 2, PASSES, P], U8, tag="scales of " + name, bufs=TILE_BUFS, align_bytes=64)
             vector.quantize_mx(
                 out=pair_codes[:].rearrange("p i c r -> p (i c r)").bitcast(E5M2),
                 scales=pair_scales[:].rearrange("p i c r -> p (i c r)"),
@@ -170,7 +182,7 @@ def tile_mlp_v1_pa_v_kernel(tc, h2, W3, b3, W4, b4, x0, x1, h3, y, grad_out, out
 
         def make_dz2(i):
             g, j = divmod(i, PACK)
-            tile_rows = ring.tile([P, OUTS], BF16, tag="dz2", bufs=3, align_bytes=64)
+            tile_rows = ring.tile([P, OUTS], BF16, tag="dz2", bufs=TILE_BUFS, align_bytes=64)
             dz2_rows[i] = tile_rows
             vector.scalar_tensor_tensor(
                 out=tile_rows[:],
@@ -186,12 +198,12 @@ def tile_mlp_v1_pa_v_kernel(tc, h2, W3, b3, W4, b4, x0, x1, h3, y, grad_out, out
             h3_rows = raw["h3", g, j // 2][:, j % 2, :]
             scalar.activation(out=h3_rows, in_=h3_rows, func=ACT.Square)
 
-        def make_dz1(i, *halves):
+        def make_dz1(i, *numbers):
             g, j = divmod(i, PACK)
             if g not in dz1_rows:
-                group_rows = ring.tile([P, PACK, HIDDEN], BF16, tag="dz1", bufs=2, align_bytes=64)
+                group_rows = ring.tile([P, PACK, HIDDEN], BF16, tag="dz1", bufs=GROUP_BUFS, align_bytes=64)
                 dz1_rows[g] = group_rows
-            for n in halves:
+            for n in numbers:
                 cols = slice(BANK * n, BANK * n + BANK)
                 vector.scalar_tensor_tensor(
                     out=dz1_rows[g][:, j, cols],
@@ -205,7 +217,7 @@ def tile_mlp_v1_pa_v_kernel(tc, h2, W3, b3, W4, b4, x0, x1, h3, y, grad_out, out
 
         def product(key, left_codes, left_scales, name, n):
             cols = slice(BANK * n, BANK * n + BANK)
-            bank = psum.tile([P, BANK], F32, tag="sums", bufs=6)
+            bank = psum.tile([P, BANK], F32, tag="sums", bufs=SUM_BANKS)
             banks[key] = bank
             for c in range(PASSES):
                 tensor.matmul_mx(
@@ -222,8 +234,8 @@ def tile_mlp_v1_pa_v_kernel(tc, h2, W3, b3, W4, b4, x0, x1, h3, y, grad_out, out
             pair_codes, pair_scales = stationary[left, i // 2]
             product(key + (i, n), pair_codes[:, i % 2], pair_scales[:, i % 2], name, n)
 
-        def make_dh(i, *halves):
-            for n in halves:
+        def make_dh(i, *numbers):
+            for n in numbers:
                 tile_product(("dh",), "dz2", i, "W4", n)
 
         def out0(i, *numbers):
@@ -233,11 +245,11 @@ def tile_mlp_v1_pa_v_kernel(tc, h2, W3, b3, W4, b4, x0, x1, h3, y, grad_out, out
         def out1(m, *numbers):
             hidden = slice(P * m, P * m + P)
             for n in numbers:
-                product(("out", 1, m, n), codes["dz1"][:, :, hidden], scales["dz1"][:, :, hidden], "h2", n)
+                product(("out", 1, m, n), codes["dz1T"][:, :, hidden], scales["dz1T"][:, :, hidden], "h2", n)
 
         def empty(output, i, n, engines):
             if (output, i) not in results:
-                result = ring.tile([P, INS], F32, tag="chunk", bufs=9, align_bytes=64)
+                result = ring.tile([P, INS], F32, tag="chunk", bufs=CHUNK_BUFS, align_bytes=64)
                 results[output, i] = result
             for k, engine in enumerate(engines):
                 cols = slice(BANK * (n + k), BANK * (n + k + 1))
@@ -249,6 +261,7 @@ def tile_mlp_v1_pa_v_kernel(tc, h2, W3, b3, W4, b4, x0, x1, h3, y, grad_out, out
         def store1(m, part):
             first, last = {"left": (0, INS // 2), "right": (INS // 2, INS), "whole": (0, INS)}[part]
             nc.sync.dma_start(out=out_1[P * m : P * m + P, first:last], in_=results[1, m][:, first:last])
+
 
         load_grad(0, 0, 1)
         load_grad(0, 1, 2)
@@ -274,6 +287,7 @@ def tile_mlp_v1_pa_v_kernel(tc, h2, W3, b3, W4, b4, x0, x1, h3, y, grad_out, out
         turn_out("dz2", 1, "s")
         load_tokens("y", 0, 2, 4)
         quantise_pair("dz2", 0)
+
         interleave("W3", 0, 0, "vsvs")
         make_dh(1, 0)
         make_dh(0, 0, 1)
@@ -308,6 +322,7 @@ def tile_mlp_v1_pa_v_kernel(tc, h2, W3, b3, W4, b4, x0, x1, h3, y, grad_out, out
         square_h3(2)
         square_h3(3)
         quantise_pair("dz1", 0)
+
         out0(0, 1)
         out0(1, 1)
         quantise("W3", 1, 2)
@@ -343,7 +358,7 @@ def tile_mlp_v1_pa_v_kernel(tc, h2, W3, b3, W4, b4, x0, x1, h3, y, grad_out, out
         empty(0, 1, 1, "ss")
         turn("dz2", 6)
         out0(2, 0)
-        interleave("dz1", 0, 0, "v")
+        interleave("dz1T", 0, 0, "v")
         turn_out("dz2", 5, "s")
         empty(0, 2, 0, "v")
         empty(0, 0, 3, "s")
@@ -372,7 +387,7 @@ def tile_mlp_v1_pa_v_kernel(tc, h2, W3, b3, W4, b4, x0, x1, h3, y, grad_out, out
         make_dh(7, 0)
         square_h3(7)
         out0(3, 1)
-        quantise("dz1", 0, 0)
+        quantise("dz1T", 0, 0)
         empty(0, 3, 1, "s")
         interleave("h2", 0, 0, "v")
         make_dh(5, 1)
@@ -396,6 +411,7 @@ def tile_mlp_v1_pa_v_kernel(tc, h2, W3, b3, W4, b4, x0, x1, h3, y, grad_out, out
         turn_out("dz1", 5, "s")
         empty(0, 2, 3, "s")
         empty(0, 3, 2, "ss")
+
         interleave("h2", 1, 0, "vs")
         quantise_pair("dz1", 2)
         out0(4, 0, 1, 2)
@@ -405,20 +421,20 @@ def tile_mlp_v1_pa_v_kernel(tc, h2, W3, b3, W4, b4, x0, x1, h3, y, grad_out, out
         out0(4, 3)
         empty(0, 4, 0, "ssss")
         empty(0, 5, 0, "s")
-        interleave("dz1", 1, 0, "v")
+        interleave("dz1T", 1, 0, "v")
         quantise("h2", 1, 0, 1)
-        store0(2)
-        store0(3)
-        store0(4)
+        for i in range(2, 5):
+            store0(i)
         out0(5, 2)
         turn("dz1", 6)
         turn("dz1", 7)
         empty(0, 5, 1, "ss")
         interleave("h2", 0, 2, "v")
-        quantise("dz1", 1, 0)
+        quantise("dz1T", 1, 0)
         interleave("h2", 0, 3, "v")
         interleave("h2", 1, 2, "v")
         out0(5, 3)
+
         out1(0, 0)
         out1(1, 0)
         out1(0, 1)
@@ -438,10 +454,8 @@ def tile_mlp_v1_pa_v_kernel(tc, h2, W3, b3, W4, b4, x0, x1, h3, y, grad_out, out
         empty(1, 2, 0, "ss")
         empty(1, 3, 0, "ss")
         store0(5)
-        store1(0, "left")
-        store1(1, "left")
-        store1(2, "left")
-        store1(3, "left")
+        for m in range(4):
+            store1(m, "left")
         quantise("h2", 1, 3)
         out1(0, 3)
         out1(1, 3)
@@ -449,21 +463,20 @@ def tile_mlp_v1_pa_v_kernel(tc, h2, W3, b3, W4, b4, x0, x1, h3, y, grad_out, out
         empty(1, 0, 2, "ss")
         empty(1, 1, 2, "ss")
         empty(1, 2, 3, "s")
-        interleave("dz1", 0, 1, "v")
-        interleave("dz1", 1, 1, "v")
-        quantise("dz1", 0, 1)
-        quantise("dz1", 1, 1)
+        interleave("dz1T", 0, 1, "v")
+        interleave("dz1T", 1, 1, "v")
+        quantise("dz1T", 0, 1)
+        quantise("dz1T", 1, 1)
         out1(3, 2, 3)
+
         out1(4, 0, 1)
         empty(1, 2, 2, "v")
         empty(1, 3, 2, "sv")
         empty(1, 4, 0, "sv")
         out1(4, 2, 3)
         out1(5, 0, 1, 2, 3)
-        store1(0, "right")
-        store1(1, "right")
-        store1(2, "right")
-        store1(3, "right")
+        for m in range(4):
+            store1(m, "right")
         turn_out("dz1", 7, "s")
         empty(1, 4, 2, "vs")
         empty(1, 5, 0, "ss")
@@ -476,9 +489,8 @@ def tile_mlp_v1_pa_v_kernel(tc, h2, W3, b3, W4, b4, x0, x1, h3, y, grad_out, out
         empty(1, 6, 1, "vvs")
         out0(7, 0, 1, 2, 3)
         empty(0, 7, 0, "vvvs")
-        store1(4, "whole")
-        store1(5, "whole")
-        store1(6, "whole")
+        for m in range(4, 7):
+            store1(m, "whole")
         store0(7)
         out1(7, 0, 1)
         out0(6, 0, 1, 2, 3)

from contextlib import ExitStack

import concourse.mybir as mybir
from concourse.masks import make_identity

TOKENS = 1024
OUTS = 1024
HIDDEN = 1024
INS = 2048

FLOPS = 2 * TOKENS * OUTS * HIDDEN + 2 * 2 * TOKENS * HIDDEN * INS
BYTES = (
    2 * (TOKENS * INS + HIDDEN * INS + OUTS * HIDDEN)
    + 2 * (TOKENS * OUTS + 2 * TOKENS)
    + 4 * (TOKENS * OUTS + TOKENS * HIDDEN)
    + 4 * (TOKENS * INS + HIDDEN * INS)
)

F32 = mybir.dt.float32
BF16 = mybir.dt.bfloat16
U32 = mybir.dt.uint32
U8 = mybir.dt.uint8
E4M3 = mybir.dt.float8_e4m3fn_x4
E5M2 = mybir.dt.float8_e5m2_x4
ALU = mybir.AluOpType
ACT = mybir.ActivationFunctionType

P = 128
PACK = 4
BANK = 512
PASSES = 2
PASS_WORDS = 256
RUN = 8

CHUNK_BUFS = 9
WHOLE_BUFS = 2
GROUPED_BUFS = 4
TILE_BUFS = 3
GROUP_BUFS = 2
TURNED_BANKS = 2
SUM_BANKS = 6


def tile_mlp_v1_pa_v_kernel(tc, h2, W3, b3, W4, b4, x0, x1, h3, y, grad_out, out_0, out_1):
    nc = tc.nc
    vector, scalar, tensor = nc.vector, nc.scalar, nc.tensor

    y_view, grad_view, h3_view, out_0_view = [
        a.rearrange("(g p j) d -> g p j d", p=P, j=PACK) for a in (y, grad_out, h3, out_0)
    ]
    weight_view = {
        name: a.rearrange("(c p t) f -> c p t f", p=P, t=PACK) for name, a in (("W4", W4), ("W3", W3), ("h2", h2))
    }

    with ExitStack() as ctx:
        keep = ctx.enter_context(tc.tile_pool(name="keep", bufs=1))
        ring = ctx.enter_context(tc.tile_pool(name="ring", bufs=1))
        psum = ctx.enter_context(tc.psum_pool(name="psum", bufs=1))
        ctx.enter_context(tc.manual_schedule())

        codes, scales = {}, {}
        for name, width in (("W4", HIDDEN), ("W3", INS), ("h2", INS), ("dz1T", HIDDEN)):
            operand_codes = keep.tile([P, PASSES, width], U32, tag="codes " + name, align_bytes=64)
            operand_scales = keep.tile([P, PASSES, width], U8, tag="scales " + name, align_bytes=64)
            codes[name], scales[name] = operand_codes, operand_scales

        identity = keep.tile([P, P], F32)
        make_identity(nc, identity[:])

        x0_sb = keep.tile([P, 2, PACK], BF16)
        x1_sb = keep.tile([P, 2, PACK], BF16)
        scalar.dma_start(out=x0_sb[:], in_=x0.rearrange("(g p j) -> p g j", p=P, j=PACK))
        scalar.dma_start(out=x1_sb[:], in_=x1.rearrange("(g p j) -> p g j", p=P, j=PACK))

        warm = keep.tile([P, 2], F32)
        vector.memset(warm[:], 0.0)
        scalar.activation(out=warm[:, 1:2], in_=warm[:, 0:1], func=ACT.Square)

        x0_row = x0_sb[:].rearrange("p g j -> p (g j)")
        x1_row = x1_sb[:].rearrange("p g j -> p (g j)")
        row_values = keep.tile([P, 7, 2 * PACK], F32)
        safe, inverse, low, low_part, high, high_part, factor = [row_values[:, r, :] for r in range(7)]
        vector.tensor_scalar(out=safe, in0=x1_row, scalar1=2.0**-126, scalar2=None, op0=ALU.max)
        vector.scalar_tensor_tensor(out=high, in0=x1_row, scalar=2.0, in1=x0_row, op0=ALU.mult, op1=ALU.subtract)
        vector.scalar_tensor_tensor(out=low, in0=x1_row, scalar=-0.5, in1=x0_row, op0=ALU.mult, op1=ALU.add)
        vector.reciprocal(out=inverse, in_=safe)
        vector.scalar_tensor_tensor(out=high_part, in0=high, scalar=0.0, in1=inverse, op0=ALU.max, op1=ALU.mult)
        vector.scalar_tensor_tensor(out=low_part, in0=low, scalar=0.0, in1=inverse, op0=ALU.max, op1=ALU.mult)
        vector.tensor_scalar(out=high_part, in0=high_part, scalar1=1.5, scalar2=-8.0, op0=ALU.min, op1=ALU.mult)
        vector.scalar_tensor_tensor(out=factor, in0=low_part, scalar=1.5, in1=high_part, op0=ALU.min, op1=ALU.mult)

        raw = {}
        dz2_rows, dz1_rows = {}, {}
        turned = {}
        features = {}
        stationary = {}
        grouped = {}
        banks = {}
        results = {}

        def copy_on(engine):
            return vector.tensor_copy if engine == "v" else scalar.copy


        def new_chunk(key, shape, dtype):
            chunk = ring.tile(shape, dtype, tag="chunk", bufs=CHUNK_BUFS, align_bytes=64)
            raw[key] = chunk

        def load_grad(g, first, last):
            if ("grad", g) not in raw:
                new_chunk(("grad", g), [P, PACK, OUTS], BF16)
            nc.sync.dma_start(out=raw["grad", g][:, first:last, :], in_=grad_view[g, :, first:last, :])

        def load_tokens(name, g, first, last):
            view = y_view if name == "y" else h3_view
            half = first // 2
            if (name, g, half) not in raw:
                new_chunk((name, g, half), [P, 2, OUTS], F32)
            nc.sync.dma_start(
                out=raw[name, g, half][:, first - 2 * half : last - 2 * half, :], in_=view[g, :, first:last, :]
            )

        def load_weight(name, c):
            if name == "W4":
                new_chunk((name, c), [P, PACK, HIDDEN], BF16)
            else:
                whole = ring.tile([P, PACK, INS], BF16, tag="whole", bufs=WHOLE_BUFS, align_bytes=64)
                raw[name, c] = whole
            nc.sync.dma_start(out=raw[name, c][:], in_=weight_view[name][c])


        def interleave(name, c, n, engines):
            for k, engine in enumerate(engines):
                cols = slice(BANK * (n + k), BANK * (n + k + 1))
                source = (dz1_rows[c] if name == "dz1T" else raw[name, c])[:, :, cols]
                columns = ring.tile([P, BANK, PACK], BF16, tag="grouped", bufs=GROUPED_BUFS, align_bytes=64)
                grouped[name, c, n + k] = columns
                copy_on(engine)(
                    out=columns[:].rearrange("p (b i) t -> p b t i", i=RUN),
                    in_=source.rearrange("p t (b i) -> p b t i", i=RUN),
                )

        def quantise(name, c, *numbers):
            for n in numbers:
                cols = slice(BANK * n, BANK * n + BANK)
                vector.quantize_mx(
                    out=codes[name][:, c, cols].bitcast(E5M2 if name == "dz1T" else E4M3),
                    scales=scales[name][:, c, cols],
                    in_=grouped[name, c, n][:].rearrange("p f t -> p (f t)"),
                )


        def turn(name, i):
            tile_rows = dz2_rows[i][:] if name == "dz2" else dz1_rows[i // PACK][:, i % PACK, :]
            bank = psum.tile([P, PASSES, 2, P], F32, tag="turned", bufs=TURNED_BANKS)
            words = tile_rows.bitcast(F32)
            for c in range(PASSES):
                for u in range(2):
                    every_second = slice(PASS_WORDS * c + u, PASS_WORDS * (c + 1), 2)
                    tensor.transpose(bank[:, c, u, :], words[:, every_second], identity[:])
            turned[name, i] = bank

        def turn_out(name, i, engine):
            if (name, i // 2) not in features:
                pair_values = ring.tile([P, 2, PASSES, P * PACK], BF16, tag="features", bufs=TILE_BUFS, align_bytes=64)
                features[name, i // 2] = pair_values
            copy_on(engine)(
                out=features[name, i // 2][:, i % 2].bitcast(F32).rearrange("p c (r u) -> p c r u", u=2),
                in_=turned[name, i][:].rearrange("p c u r -> p c r u"),
            )

        def quantise_pair(name, pair):
            pair_codes = ring.tile([P, 2, PASSES, P], U32, tag="codes of " + name, bufs=TILE_BUFS, align_bytes=64)
            pair_scales = ring.tile([P, 2, PASSES, P], U8, tag="scales of " + name, bufs=TILE_BUFS, align_bytes=64)
            vector.quantize_mx(
                out=pair_codes[:].rearrange("p i c r -> p (i c r)").bitcast(E5M2),
                scales=pair_scales[:].rearrange("p i c r -> p (i c r)"),
                in_=features[name, pair][:].rearrange("p i c w -> p (i c w)"),
            )
            stationary[name, pair] = (pair_codes, pair_scales)


        def make_dz2(i):
            g, j = divmod(i, PACK)
            tile_rows = ring.tile([P, OUTS], BF16, tag="dz2", bufs=TILE_BUFS, align_bytes=64)
            dz2_rows[i] = tile_rows
            vector.scalar_tensor_tensor(
                out=tile_rows[:],
                in0=raw["y", g, j // 2][:, j % 2, :],
                scalar=factor[:, i : i + 1],
                in1=raw["grad", g][:, j, :],
                op0=ALU.mult,
                op1=ALU.mult,
            )

        def square_h3(i):
            g, j = divmod(i, PACK)
            h3_rows = raw["h3", g, j // 2][:, j % 2, :]
            scalar.activation(out=h3_rows, in_=h3_rows, func=ACT.Square)

        def make_dz1(i, *numbers):
            g, j = divmod(i, PACK)
            if g not in dz1_rows:
                group_rows = ring.tile([P, PACK, HIDDEN], BF16, tag="dz1", bufs=GROUP_BUFS, align_bytes=64)
                dz1_rows[g] = group_rows
            for n in numbers:
                cols = slice(BANK * n, BANK * n + BANK)
                vector.scalar_tensor_tensor(
                    out=dz1_rows[g][:, j, cols],
                    in0=raw["h3", g, j // 2][:, j % 2, cols],
                    scalar=1.0,
                    in1=banks["dh", i, n][:],
                    op0=ALU.subtract,
                    op1=ALU.mult,
                )


        def product(key, left_codes, left_scales, name, n):
            cols = slice(BANK * n, BANK * n + BANK)
            bank = psum.tile([P, BANK], F32, tag="sums", bufs=SUM_BANKS)
            banks[key] = bank
            for c in range(PASSES):
                tensor.matmul_mx(
                    out=bank[:],
                    lhsT=left_codes[:, c, :].bitcast(E5M2),
                    lhsT_scale=left_scales[:, c, :],
                    rhs=codes[name][:, c, cols].bitcast(E4M3),
                    rhs_scale=scales[name][:, c, cols],
                    start=(c == 0),
                    stop=(c == PASSES - 1),
                )

        def tile_product(key, left, i, name, n):
            pair_codes, pair_scales = stationary[left, i // 2]
            product(key + (i, n), pair_codes[:, i % 2], pair_scales[:, i % 2], name, n)

        def make_dh(i, *numbers):
            for n in numbers:
                tile_product(("dh",), "dz2", i, "W4", n)

        def out0(i, *numbers):
            for n in numbers:
                tile_product(("out", 0), "dz1", i, "W3", n)

        def out1(m, *numbers):
            hidden = slice(P * m, P * m + P)
            for n in numbers:
                product(("out", 1, m, n), codes["dz1T"][:, :, hidden], scales["dz1T"][:, :, hidden], "h2", n)

        def empty(output, i, n, engines):
            if (output, i) not in results:
                result = ring.tile([P, INS], F32, tag="chunk", bufs=CHUNK_BUFS, align_bytes=64)
                results[output, i] = result
            for k, engine in enumerate(engines):
                cols = slice(BANK * (n + k), BANK * (n + k + 1))
                copy_on(engine)(out=results[output, i][:, cols], in_=banks["out", output, i, n + k][:])

        def store0(i):
            nc.sync.dma_start(out=out_0_view[i // PACK, :, i % PACK, :], in_=results[0, i][:])

        def store1(m, part):
            first, last = {"left": (0, INS // 2), "right": (INS // 2, INS), "whole": (0, INS)}[part]
            nc.sync.dma_start(out=out_1[P * m : P * m + P, first:last], in_=results[1, m][:, first:last])


        load_grad(0, 0, 1)
        load_grad(0, 1, 2)
        load_weight("W4", 0)
        load_weight("W4", 1)
        interleave("W4", 0, 1, "s")
        interleave("W4", 1, 1, "v")
        interleave("W4", 1, 0, "s")
        interleave("W4", 0, 0, "s")
        load_tokens("y", 0, 0, 1)
        load_tokens("y", 0, 1, 2)
        make_dz2(0)
        make_dz2(1)
        quantise("W4", 1, 1)
        quantise("W4", 1, 0)
        quantise("W4", 0, 1)
        quantise("W4", 0, 0)
        turn("dz2", 0)
        turn("dz2", 1)
        load_weight("W3", 0)
        load_grad(0, 2, 4)
        turn_out("dz2", 0, "s")
        turn_out("dz2", 1, "s")
        load_tokens("y", 0, 2, 4)
        quantise_pair("dz2", 0)

        interleave("W3", 0, 0, "vsvs")
        make_dh(1, 0)
        make_dh(0, 0, 1)
        quantise("W3", 0, 0, 1)
        make_dz2(2)
        make_dz2(3)
        quantise("W3", 0, 2, 3)
        load_tokens("h3", 0, 0, 2)
        square_h3(0)
        square_h3(1)
        make_dz1(0, 0, 1)
        make_dz1(1, 0)
        load_weight("W3", 1)
        load_tokens("h3", 0, 2, 4)
        turn("dz2", 2)
        turn_out("dz2", 2, "s")
        make_dh(1, 1)
        turn("dz2", 3)
        turn("dz1", 0)
        turn_out("dz2", 3, "s")
        make_dz1(1, 1)
        quantise_pair("dz2", 1)
        turn_out("dz1", 0, "s")
        interleave("W3", 1, 1, "s")
        interleave("W3", 1, 0, "v")
        interleave("W3", 1, 2, "v")
        turn("dz1", 1)
        make_dh(2, 0, 1)
        make_dh(3, 0, 1)
        quantise("W3", 1, 0, 1)
        turn_out("dz1", 1, "s")
        square_h3(2)
        square_h3(3)
        quantise_pair("dz1", 0)

        out0(0, 1)
        out0(1, 1)
        quantise("W3", 1, 2)
        make_dz1(2, 0, 1)
        make_dz1(3, 0, 1)
        load_tokens("y", 1, 0, 2)
        load_grad(1, 0, 4)
        make_dz2(4)
        make_dz2(5)
        out0(1, 0)
        turn("dz1", 2)
        turn("dz1", 3)
        interleave("W3", 1, 3, "s")
        out0(0, 0)
        out0(0, 2)
        empty(0, 0, 1, "s")
        turn_out("dz1", 2, "s")
        load_tokens("y", 1, 2, 4)
        empty(0, 1, 0, "s")
        turn_out("dz1", 3, "s")
        empty(0, 0, 0, "s")
        empty(0, 0, 2, "s")
        quantise_pair("dz1", 1)
        turn("dz2", 4)
        out0(1, 2)
        quantise("W3", 1, 3)
        make_dz2(6)
        make_dz2(7)
        load_tokens("h3", 1, 0, 2)
        out0(0, 3)
        turn("dz2", 5)
        turn_out("dz2", 4, "s")
        empty(0, 1, 1, "ss")
        turn("dz2", 6)
        out0(2, 0)
        interleave("dz1T", 0, 0, "v")
        turn_out("dz2", 5, "s")
        empty(0, 2, 0, "v")
        empty(0, 0, 3, "s")
        turn("dz2", 7)
        out0(1, 3)
        out0(3, 0)
        out0(2, 1)
        quantise_pair("dz2", 2)
        make_dh(5, 0)
        make_dh(4, 0, 1)
        load_weight("h2", 0)
        turn_out("dz2", 6, "s")
        turn_out("dz2", 7, "v")
        square_h3(4)
        square_h3(5)
        empty(0, 1, 3, "v")
        empty(0, 3, 0, "s")
        empty(0, 2, 1, "s")
        quantise_pair("dz2", 3)
        make_dz1(5, 0)
        make_dz1(4, 0)
        load_tokens("h3", 1, 2, 4)
        out0(2, 2)
        interleave("h2", 0, 1, "s")
        empty(0, 2, 2, "s")
        make_dh(7, 0)
        square_h3(7)
        out0(3, 1)
        quantise("dz1T", 0, 0)
        empty(0, 3, 1, "s")
        interleave("h2", 0, 0, "v")
        make_dh(5, 1)
        make_dz1(4, 1)
        make_dz1(5, 1)
        quantise("h2", 0, 0, 1)
        load_weight("h2", 1)
        store0(1)
        store0(0)
        out0(3, 2)
        turn("dz1", 4)
        turn("dz1", 5)
        out0(2, 3)
        out0(3, 3)
        make_dz1(7, 0)
        make_dh(6, 0)
        make_dh(7, 1)
        make_dh(6, 1)
        square_h3(6)
        turn_out("dz1", 4, "s")
        turn_out("dz1", 5, "s")
        empty(0, 2, 3, "s")
        empty(0, 3, 2, "ss")

        interleave("h2", 1, 0, "vs")
        quantise_pair("dz1", 2)
        out0(4, 0, 1, 2)
        make_dz1(7, 1)
        make_dz1(6, 0, 1)
        out0(5, 0, 1)
        out0(4, 3)
        empty(0, 4, 0, "ssss")
        empty(0, 5, 0, "s")
        interleave("dz1T", 1, 0, "v")
        quantise("h2", 1, 0, 1)
        for i in range(2, 5):
            store0(i)
        out0(5, 2)
        turn("dz1", 6)
        turn("dz1", 7)
        empty(0, 5, 1, "ss")
        interleave("h2", 0, 2, "v")
        quantise("dz1T", 1, 0)
        interleave("h2", 0, 3, "v")
        interleave("h2", 1, 2, "v")
        out0(5, 3)

        out1(0, 0)
        out1(1, 0)
        out1(0, 1)
        out1(1, 1)
        out1(2, 0)
        empty(0, 5, 3, "s")
        empty(1, 0, 0, "sv")
        empty(1, 1, 0, "sv")
        out1(3, 0, 1)
        out1(2, 1)
        quantise("h2", 0, 2)
        quantise("h2", 1, 2)
        quantise("h2", 0, 3)
        out1(0, 2)
        out1(1, 2)
        interleave("h2", 1, 3, "s")
        empty(1, 2, 0, "ss")
        empty(1, 3, 0, "ss")
        store0(5)
        for m in range(4):
            store1(m, "left")
        quantise("h2", 1, 3)
        out1(0, 3)
        out1(1, 3)
        out1(2, 2, 3)
        empty(1, 0, 2, "ss")
        empty(1, 1, 2, "ss")
        empty(1, 2, 3, "s")
        interleave("dz1T", 0, 1, "v")
        interleave("dz1T", 1, 1, "v")
        quantise("dz1T", 0, 1)
        quantise("dz1T", 1, 1)
        out1(3, 2, 3)

        out1(4, 0, 1)
        empty(1, 2, 2, "v")
        empty(1, 3, 2, "sv")
        empty(1, 4, 0, "sv")
        out1(4, 2, 3)
        out1(5, 0, 1, 2, 3)
        for m in range(4):
            store1(m, "right")
        turn_out("dz1", 7, "s")
        empty(1, 4, 2, "vs")
        empty(1, 5, 0, "ss")
        empty(1, 5, 3, "s")
        out1(6, 0, 1, 2, 3)
        turn_out("dz1", 6, "v")
        quantise_pair("dz1", 3)
        empty(1, 6, 0, "s")
        empty(1, 5, 2, "v")
        empty(1, 6, 1, "vvs")
        out0(7, 0, 1, 2, 3)
        empty(0, 7, 0, "vvvs")
        for m in range(4, 7):
            store1(m, "whole")
        store0(7)
        out1(7, 0, 1)
        out0(6, 0, 1, 2, 3)
        empty(1, 7, 1, "s")
        empty(0, 6, 0, "v")
        empty(1, 7, 0, "v")
        empty(0, 6, 1, "ssv")
        out1(7, 2, 3)
        store1(7, "left")
        store0(6)
        empty(1, 7, 2, "ss")
        store1(7, "right")
